import numpy as np
import ml_dtypes


def mxq(x, axis, fmt="e4m3"):
    dtype, down = {"e4m3": (ml_dtypes.float8_e4m3fn, 7), "e5m2": (ml_dtypes.float8_e5m2, 14)}[fmt]
    v = np.moveaxis(np.asarray(x, np.float32).astype(ml_dtypes.bfloat16).astype(np.float64), axis, -1)
    blocks = v.reshape(v.shape[:-1] + (-1, 32))
    amax = np.abs(blocks).max(-1, keepdims=True)
    byte = np.maximum(np.where(amax > 0, np.frexp(amax)[1] - 1 + 127, 0) - down, 1)
    scale = np.exp2(byte - 127.0)
    codes = (blocks / scale).astype(np.float32).astype(dtype).astype(np.float64)
    return np.moveaxis((codes * scale).reshape(v.shape), -1, axis)


WIDE = False


def mx_kscale(k):
    if not WIDE:
        return np.ones(k)
    levels = np.array([10, -10, 5, -5, 0])
    a = np.random.permutation(np.resize(levels, k // 512 * 4)).reshape(k // 512, 4)
    idx = np.arange(k)
    return np.exp2(a[idx // 512, idx % 128 // 32])


BF16 = ml_dtypes.bfloat16


def bf(x):
    return np.asarray(x, np.float32).astype(BF16)


def f64(x):
    return np.asarray(x).astype(np.float64)


M, J, L, H, K, I, S = 8, 512, 28, 28, 3, 128, 2
SHIFT = 1


def setup_inputs():
    s = mx_kscale(J)
    x = np.random.standard_normal((M, J, L, H)) * s[None, :, None, None]
    return {"x": bf(x.reshape(M, J * L, H)),
            "w1": bf(np.random.standard_normal((I, S))),
            "w2": bf(np.random.standard_normal((J, K, I)) / np.sqrt(J * K) / s[:, None, None])}


def reference(x, w1, w2):
    xq = mxq(f64(x).reshape(M, J, L, H).transpose(0, 2, 3, 1).reshape(M * L * H, J), 1, "e4m3")
    y = [(xq @ mxq(f64(w2)[:, k, :], 0, "e4m3")).reshape(M, L, H, I) for k in range(K)]
    t4 = sum(np.pad(y[k], ((0, 0), (0, 0), (1, 1), (0, 0)))[:, :, k:k + H, :] for k in range(K))
    t5 = t4[..., None] * f64(w1)
    t6 = np.roll(t5, SHIFT, axis=1)
    t6 = np.transpose(t6, (0, 2, 3, 1, 4)).reshape(M, H, I, L * S)
    t6 = np.roll(t6, SHIFT, axis=3)
    t6 = t6.reshape(M, H, I, L, S).sum(axis=4)
    return np.transpose(t6, (0, 2, 3, 1))

@@ -1,0 +1,195 @@
+from contextlib import ExitStack
+
+import concourse.mybir as mybir
+
+FLOPS = 2 * 8 * 28 * 28 * 512 * 3 * 128
+
+BF16 = mybir.dt.bfloat16
+F32 = mybir.dt.float32
+I32 = mybir.dt.int32
+U32 = mybir.dt.uint32
+U8 = mybir.dt.uint8
+FP8X4 = mybir.dt.float8_e4m3fn_x4
+COPY = mybir.ActivationFunctionType.Copy
+MULT = mybir.AluOpType.mult
+ADD = mybir.AluOpType.add
+
+P = 128
+PACK = 4
+M, L, H, K, I = 8, 28, 28, 3, 128
+MC = 2
+NQ = M // MC
+G = 64
+GU = MC * L
+NP = H + 2
+NBLOCKS = ((0, 8), (8, 8), (16, 8), (24, 4))
+NV = (16, 12, 16, 12)
+PINNED = False
+
+
+def pieces(n_lo, n_hi):
+    cut = []
+    at = n_lo
+    while at < n_hi:
+        for size in (16, 8, 4):
+            if at + size <= n_hi:
+                cut.append((at, size))
+                at += size
+                break
+    return cut
+
+
+def tile_kernel_generated_1_kernel(tc, x, w1, w2, out):
+    nc = tc.nc
+    with ExitStack() as ctx:
+        keep = ctx.enter_context(tc.tile_pool(name="keep", bufs=1))
+        bpool = ctx.enter_context(tc.tile_pool(name="bpool", bufs=4))
+        psum = ctx.enter_context(tc.psum_pool(name="psum", bufs=8))
+        if PINNED:
+            ctx.enter_context(tc.manual_schedule())
+
+        xr = [keep.tile([P, PACK, L, H], BF16, name="xr%d" % m) for m in range(M)]
+        wr = keep.tile([P, PACK, K * I], BF16, name="wr")
+        wg = keep.tile([P, K * I, PACK], BF16, name="wg", align_bytes=64)
+        wcodes = keep.tile([P, K * I], U32, name="wcodes", align_bytes=64)
+        wscales = keep.tile([P, K * I], U8, name="wscales", align_bytes=64)
+        w1b = keep.tile([P, 2], BF16, name="w1b")
+        w1f = keep.tile([P, 2], F32, name="w1f")
+        warm = keep.tile([P, 2], F32, name="warm")
+        gv = [keep.tile([P, NV[q], G, PACK], BF16, name="gv%d" % q, align_bytes=64) for q in range(NQ)]
+        gs = [keep.tile([P, H - NV[q], G, PACK], BF16, name="gs%d" % q, align_bytes=64) for q in range(NQ)]
+        codes = [keep.tile([P, NP * G], U32, name="codes%d" % q, align_bytes=64) for q in range(NQ)]
+        scales = [keep.tile([P, NP * G], U8, name="scales%d" % q, align_bytes=64) for q in range(NQ)]
+        ot = [keep.tile([P, MC, L, H], F32, name="ot%d" % q) for q in range(NQ)]
+
+        nc.scalar.dma_start(out=w1b[:], in_=w1)
+        nc.scalar.dma_start(
+            out=wr[:].rearrange("p j c -> p (j c)"),
+            in_=w2.rearrange("(p j) k i -> p (j k i)", j=PACK),
+        )
+        for m in range(M):
+            nc.sync.dma_start(
+                out=xr[m][:].rearrange("p j l n -> p (j l n)"),
+                in_=x[m].rearrange("(p r) n -> p (r n)", p=P),
+            )
+
+        nc.vector.memset(warm[:, 0:1], 0.0)
+        nc.scalar.activation(out=warm[:, 1:2], in_=warm[:, 0:1], func=COPY, scale=1.0)
+        for q in range(NQ):
+            nc.vector.memset(gv[q][:, :, GU:G, :], 0.0)
+            nc.vector.memset(gs[q][:, :, GU:G, :], 0.0)
+            for row in (0, NP - 1):
+                nc.vector.memset(codes[q][:, row * G : (row + 1) * G].bitcast(I32), 0)
+                nc.vector.memset(scales[q][:, row * G : (row + 1) * G].bitcast(I32), 0)
+        nc.vector.tensor_copy(out=w1f[:], in_=w1b[:])
+
+        def weights():
+            nc.vector.tensor_copy(
+                out=wg[:].rearrange("p (c i) j -> p c j i", i=4),
+                in_=wr[:].rearrange("p j (c i) -> p c j i", i=4),
+            )
+            flat = wg[:].rearrange("p c j -> p (c j)")
+            for lo, hi in ((0, 256), (256, 384)):
+                nc.vector.quantize_mx(
+                    out=wcodes[:, lo:hi].bitcast(FP8X4),
+                    scales=wscales[:, lo:hi],
+                    in_=flat[:, lo * PACK : hi * PACK],
+                )
+
+        def regroup_vector(q, mm):
+            nc.vector.tensor_copy(
+                out=gv[q][:, :, mm * L : (mm + 1) * L, :].rearrange("p (c i) l j -> p c l j i", i=4),
+                in_=xr[q * MC + mm][:, :, :, 0 : NV[q]].rearrange("p j l (c i) -> p c l j i", i=4),
+            )
+
+        def regroup_scalar(q, mm):
+            for c in range((H - NV[q]) // 4):
+                nc.scalar.copy(
+                    out=gs[q][:, 4 * c : 4 * c + 4, mm * L : (mm + 1) * L, :].rearrange("p i l j -> p l j i"),
+                    in_=xr[q * MC + mm][:, :, :, NV[q] + 4 * c : NV[q] + 4 * c + 4].rearrange("p j l i -> p l j i"),
+                )
+
+        def quantise(q, src, n_base, n_lo, n_hi):
+            for at, size in pieces(n_lo, n_hi):
+                cols = slice((at + 1) * G, (at + 1 + size) * G)
+                nc.vector.quantize_mx(
+                    out=codes[q][:, cols].bitcast(FP8X4),
+                    scales=scales[q][:, cols],
+                    in_=src[:, at - n_base : at - n_base + size].rearrange("p n g j -> p (n g j)"),
+                )
+
+        def quantise_vector(q):
+            quantise(q, gv[q], 0, 0, NV[q])
+
+        def quantise_scalar(q):
+            quantise(q, gs[q], NV[q], NV[q], H)
+
+        accs = {}
+
+        def multiply(q, b):
+            n0, nn = NBLOCKS[b]
+            acc = psum.tile([P, 512], F32, name="acc")
+            accs[(q, b)] = acc
+            for k in range(K):
+                cols = slice((n0 + k) * G, (n0 + k + nn) * G)
+                nc.tensor.matmul_mx(
+                    out=acc[:, 0 : nn * G],
+                    lhsT=wcodes[:, k * I : (k + 1) * I].bitcast(FP8X4),
+                    lhsT_scale=wscales[:, k * I : (k + 1) * I],
+                    rhs=codes[q][:, cols].bitcast(FP8X4),
+                    rhs_scale=scales[q][:, cols],
+                    start=(k == 0),
+                    stop=(k == K - 1),
+                )
+
+        bts = {}
+
+        def second_term(q, b):
+            n0, nn = NBLOCKS[b]
+            t4 = accs[(q, b)][:, 0 : nn * G].rearrange("p (n g) -> p g n", g=G)
+            bt = bpool.tile([P, GU, 8], F32, name="bt")
+            bts[(q, b)] = bt
+            nc.scalar.activation(out=bt[:, 1:GU, 0:nn], in_=t4[:, 0 : GU - 1, :], func=COPY, scale=w1f[:, 1:2])
+            nc.scalar.activation(out=bt[:, 0:GU:L, 0:nn], in_=t4[:, L - 1 : GU : L, :], func=COPY, scale=w1f[:, 1:2])
+
+        def first_term(q, b):
+            n0, nn = NBLOCKS[b]
+            t4 = accs[(q, b)][:, 0 : nn * G].rearrange("p (n g) -> p g n", g=G)
+            nc.vector.scalar_tensor_tensor(
+                out=ot[q][:].rearrange("p m l n -> p (m l) n")[:, :, n0 : n0 + nn],
+                in0=t4[:, 0:GU, :],
+                scalar=w1f[:, 0:1],
+                in1=bts[(q, b)][:, :, 0:nn],
+                op0=MULT,
+                op1=ADD,
+            )
+
+        def store(q):
+            ms = slice(q * MC, (q + 1) * MC)
+            nc.sync.dma_start(
+                out=out[ms, :, 0, :].rearrange("m i n -> i m n"),
+                in_=ot[q][:, :, L - 1, :],
+            )
+            nc.sync.dma_start(
+                out=out[ms, :, 1:L, :].rearrange("m i l n -> i m (l n)"),
+                in_=ot[q][:, :, 0 : L - 1, :].rearrange("p m l n -> p m (l n)"),
+            )
+
+        def epilogue(q):
+            for b in range(len(NBLOCKS)):
+                second_term(q, b)
+                first_term(q, b)
+            store(q)
+
+        weights()
+        for q in range(NQ + 1):
+            if q < NQ:
+                for mm in range(MC):
+                    regroup_vector(q, mm)
+                    regroup_scalar(q, mm)
+                quantise_vector(q)
+                quantise_scalar(q)
+                for b in range(len(NBLOCKS)):
+                    multiply(q, b)
+            if q >= 1:
+                epilogue(q - 1)

@@ -24,7 +24,7 @@ GU = MC * L
 NP = H + 2
 NBLOCKS = ((0, 8), (8, 8), (16, 8), (24, 4))
 NV = (16, 12, 16, 12)
-PINNED = False
+PINNED = True
 
 
 def pieces(n_lo, n_hi):
@@ -63,15 +63,16 @@ def tile_kernel_generated_1_kernel(tc, x, w1, w2, out):
         ot = [keep.tile([P, MC, L, H], F32, name="ot%d" % q) for q in range(NQ)]
 
         nc.scalar.dma_start(out=w1b[:], in_=w1)
-        nc.scalar.dma_start(
-            out=wr[:].rearrange("p j c -> p (j c)"),
-            in_=w2.rearrange("(p j) k i -> p (j k i)", j=PACK),
-        )
         for m in range(M):
             nc.sync.dma_start(
                 out=xr[m][:].rearrange("p j l n -> p (j l n)"),
                 in_=x[m].rearrange("(p r) n -> p (r n)", p=P),
             )
+            if m == 1:
+                nc.sync.dma_start(
+                    out=wr[:].rearrange("p j c -> p (j c)"),
+                    in_=w2.rearrange("(p j) k i -> p (j k i)", j=PACK),
+                )
 
         nc.vector.memset(warm[:, 0:1], 0.0)
         nc.scalar.activation(out=warm[:, 1:2], in_=warm[:, 0:1], func=COPY, scale=1.0)
@@ -181,12 +182,13 @@ def tile_kernel_generated_1_kernel(tc, x, w1, w2, out):
                 first_term(q, b)
             store(q)
 
-        weights()
         for q in range(NQ + 1):
             if q < NQ:
                 for mm in range(MC):
                     regroup_vector(q, mm)
                     regroup_scalar(q, mm)
+                if q == 0:
+                    weights()
                 quantise_vector(q)
                 quantise_scalar(q)
                 for b in range(len(NBLOCKS)):

@@ -63,25 +63,25 @@ def tile_kernel_generated_1_kernel(tc, x, w1, w2, out):
         ot = [keep.tile([P, MC, L, H], F32, name="ot%d" % q) for q in range(NQ)]
 
         nc.scalar.dma_start(out=w1b[:], in_=w1)
+        nc.sync.dma_start(
+            out=wr[:].rearrange("p j c -> p (j c)"),
+            in_=w2.rearrange("(p j) k i -> p (j k i)", j=PACK),
+        )
         for m in range(M):
             nc.sync.dma_start(
                 out=xr[m][:].rearrange("p j l n -> p (j l n)"),
                 in_=x[m].rearrange("(p r) n -> p (r n)", p=P),
             )
-            if m == 1:
-                nc.sync.dma_start(
-                    out=wr[:].rearrange("p j c -> p (j c)"),
-                    in_=w2.rearrange("(p j) k i -> p (j k i)", j=PACK),
-                )
 
         nc.vector.memset(warm[:, 0:1], 0.0)
         nc.scalar.activation(out=warm[:, 1:2], in_=warm[:, 0:1], func=COPY, scale=1.0)
         for q in range(NQ):
-            nc.vector.memset(gv[q][:, :, GU:G, :], 0.0)
-            nc.vector.memset(gs[q][:, :, GU:G, :], 0.0)
-            for row in (0, NP - 1):
-                nc.vector.memset(codes[q][:, row * G : (row + 1) * G].bitcast(I32), 0)
-                nc.vector.memset(scales[q][:, row * G : (row + 1) * G].bitcast(I32), 0)
+            eng = nc.vector
+            edge = slice(0, NP, NP - 1)
+            eng.memset(gv[q][:, :, GU:G, :].rearrange("p n g j -> p n (g j)").bitcast(F32), 0.0)
+            eng.memset(gs[q][:, :, GU:G, :].rearrange("p n g j -> p n (g j)").bitcast(F32), 0.0)
+            eng.memset(codes[q][:].rearrange("p (r g) -> p r g", g=G)[:, edge, :].bitcast(F32), 0.0)
+            eng.memset(scales[q][:].rearrange("p (r g) -> p r g", g=G)[:, edge, :].bitcast(F32), 0.0)
         nc.vector.tensor_copy(out=w1f[:], in_=w1b[:])
 
         def weights():
@@ -98,10 +98,11 @@ def tile_kernel_generated_1_kernel(tc, x, w1, w2, out):
                 )
 
         def regroup_vector(q, mm):
-            nc.vector.tensor_copy(
-                out=gv[q][:, :, mm * L : (mm + 1) * L, :].rearrange("p (c i) l j -> p c l j i", i=4),
-                in_=xr[q * MC + mm][:, :, :, 0 : NV[q]].rearrange("p j l (c i) -> p c l j i", i=4),
-            )
+            for at, size in pieces(0, NV[q]):
+                nc.vector.tensor_copy(
+                    out=gv[q][:, at : at + size, mm * L : (mm + 1) * L, :].rearrange("p (c i) l j -> p c l j i", i=4),
+                    in_=xr[q * MC + mm][:, :, :, at : at + size].rearrange("p j l (c i) -> p c l j i", i=4),
+                )
 
         def regroup_scalar(q, mm):
             for c in range((H - NV[q]) // 4):
@@ -182,13 +183,12 @@ def tile_kernel_generated_1_kernel(tc, x, w1, w2, out):
                 first_term(q, b)
             store(q)
 
+        weights()
         for q in range(NQ + 1):
             if q < NQ:
                 for mm in range(MC):
                     regroup_vector(q, mm)
                     regroup_scalar(q, mm)
-                if q == 0:
-                    weights()
                 quantise_vector(q)
                 quantise_scalar(q)
                 for b in range(len(NBLOCKS)):

@@ -23,7 +23,7 @@ G = 64
 GU = MC * L
 NP = H + 2
 NBLOCKS = ((0, 8), (8, 8), (16, 8), (24, 4))
-NV = (16, 12, 16, 12)
+NV = (16, 16, 16, 16)
 PINNED = True
 
 

from contextlib import ExitStack

import concourse.mybir as mybir

FLOPS = 2 * 8 * 28 * 28 * 512 * 3 * 128

BF16 = mybir.dt.bfloat16
F32 = mybir.dt.float32
I32 = mybir.dt.int32
U32 = mybir.dt.uint32
U8 = mybir.dt.uint8
FP8X4 = mybir.dt.float8_e4m3fn_x4
COPY = mybir.ActivationFunctionType.Copy
MULT = mybir.AluOpType.mult
ADD = mybir.AluOpType.add

P = 128
PACK = 4
M, L, H, K, I = 8, 28, 28, 3, 128
MC = 2
NQ = M // MC
G = 64
GU = MC * L
NP = H + 2
NBLOCKS = ((0, 8), (8, 8), (16, 8), (24, 4))
NV = (16, 16, 16, 16)
PINNED = True


def pieces(n_lo, n_hi):
    cut = []
    at = n_lo
    while at < n_hi:
        for size in (16, 8, 4):
            if at + size <= n_hi:
                cut.append((at, size))
                at += size
                break
    return cut


def tile_kernel_generated_1_kernel(tc, x, w1, w2, out):
    nc = tc.nc
    with ExitStack() as ctx:
        keep = ctx.enter_context(tc.tile_pool(name="keep", bufs=1))
        bpool = ctx.enter_context(tc.tile_pool(name="bpool", bufs=4))
        psum = ctx.enter_context(tc.psum_pool(name="psum", bufs=8))
        if PINNED:
            ctx.enter_context(tc.manual_schedule())

        xr = [keep.tile([P, PACK, L, H], BF16, name="xr%d" % m) for m in range(M)]
        wr = keep.tile([P, PACK, K * I], BF16, name="wr")
        wg = keep.tile([P, K * I, PACK], BF16, name="wg", align_bytes=64)
        wcodes = keep.tile([P, K * I], U32, name="wcodes", align_bytes=64)
        wscales = keep.tile([P, K * I], U8, name="wscales", align_bytes=64)
        w1b = keep.tile([P, 2], BF16, name="w1b")
        w1f = keep.tile([P, 2], F32, name="w1f")
        warm = keep.tile([P, 2], F32, name="warm")
        gv = [keep.tile([P, NV[q], G, PACK], BF16, name="gv%d" % q, align_bytes=64) for q in range(NQ)]
        gs = [keep.tile([P, H - NV[q], G, PACK], BF16, name="gs%d" % q, align_bytes=64) for q in range(NQ)]
        codes = [keep.tile([P, NP * G], U32, name="codes%d" % q, align_bytes=64) for q in range(NQ)]
        scales = [keep.tile([P, NP * G], U8, name="scales%d" % q, align_bytes=64) for q in range(NQ)]
        ot = [keep.tile([P, MC, L, H], F32, name="ot%d" % q) for q in range(NQ)]

        nc.scalar.dma_start(out=w1b[:], in_=w1)
        nc.sync.dma_start(
            out=wr[:].rearrange("p j c -> p (j c)"),
            in_=w2.rearrange("(p j) k i -> p (j k i)", j=PACK),
        )
        for m in range(M):
            nc.sync.dma_start(
                out=xr[m][:].rearrange("p j l n -> p (j l n)"),
                in_=x[m].rearrange("(p r) n -> p (r n)", p=P),
            )

        nc.vector.memset(warm[:, 0:1], 0.0)
        nc.scalar.activation(out=warm[:, 1:2], in_=warm[:, 0:1], func=COPY, scale=1.0)
        for q in range(NQ):
            eng = nc.vector
            edge = slice(0, NP, NP - 1)
            eng.memset(gv[q][:, :, GU:G, :].rearrange("p n g j -> p n (g j)").bitcast(F32), 0.0)
            eng.memset(gs[q][:, :, GU:G, :].rearrange("p n g j -> p n (g j)").bitcast(F32), 0.0)
            eng.memset(codes[q][:].rearrange("p (r g) -> p r g", g=G)[:, edge, :].bitcast(F32), 0.0)
            eng.memset(scales[q][:].rearrange("p (r g) -> p r g", g=G)[:, edge, :].bitcast(F32), 0.0)
        nc.vector.tensor_copy(out=w1f[:], in_=w1b[:])

        def weights():
            nc.vector.tensor_copy(
                out=wg[:].rearrange("p (c i) j -> p c j i", i=4),
                in_=wr[:].rearrange("p j (c i) -> p c j i", i=4),
            )
            flat = wg[:].rearrange("p c j -> p (c j)")
            for lo, hi in ((0, 256), (256, 384)):
                nc.vector.quantize_mx(
                    out=wcodes[:, lo:hi].bitcast(FP8X4),
                    scales=wscales[:, lo:hi],
                    in_=flat[:, lo * PACK : hi * PACK],
                )

        def regroup_vector(q, mm):
            for at, size in pieces(0, NV[q]):
                nc.vector.tensor_copy(
                    out=gv[q][:, at : at + size, mm * L : (mm + 1) * L, :].rearrange("p (c i) l j -> p c l j i", i=4),
                    in_=xr[q * MC + mm][:, :, :, at : at + size].rearrange("p j l (c i) -> p c l j i", i=4),
                )

        def regroup_scalar(q, mm):
            for c in range((H - NV[q]) // 4):
                nc.scalar.copy(
                    out=gs[q][:, 4 * c : 4 * c + 4, mm * L : (mm + 1) * L, :].rearrange("p i l j -> p l j i"),
                    in_=xr[q * MC + mm][:, :, :, NV[q] + 4 * c : NV[q] + 4 * c + 4].rearrange("p j l i -> p l j i"),
                )

        def quantise(q, src, n_base, n_lo, n_hi):
            for at, size in pieces(n_lo, n_hi):
                cols = slice((at + 1) * G, (at + 1 + size) * G)
                nc.vector.quantize_mx(
                    out=codes[q][:, cols].bitcast(FP8X4),
                    scales=scales[q][:, cols],
                    in_=src[:, at - n_base : at - n_base + size].rearrange("p n g j -> p (n g j)"),
                )

        def quantise_vector(q):
            quantise(q, gv[q], 0, 0, NV[q])

        def quantise_scalar(q):
            quantise(q, gs[q], NV[q], NV[q], H)

        accs = {}

        def multiply(q, b):
            n0, nn = NBLOCKS[b]
            acc = psum.tile([P, 512], F32, name="acc")
            accs[(q, b)] = acc
            for k in range(K):
                cols = slice((n0 + k) * G, (n0 + k + nn) * G)
                nc.tensor.matmul_mx(
                    out=acc[:, 0 : nn * G],
                    lhsT=wcodes[:, k * I : (k + 1) * I].bitcast(FP8X4),
                    lhsT_scale=wscales[:, k * I : (k + 1) * I],
                    rhs=codes[q][:, cols].bitcast(FP8X4),
                    rhs_scale=scales[q][:, cols],
                    start=(k == 0),
                    stop=(k == K - 1),
                )

        bts = {}

        def second_term(q, b):
            n0, nn = NBLOCKS[b]
            t4 = accs[(q, b)][:, 0 : nn * G].rearrange("p (n g) -> p g n", g=G)
            bt = bpool.tile([P, GU, 8], F32, name="bt")
            bts[(q, b)] = bt
            nc.scalar.activation(out=bt[:, 1:GU, 0:nn], in_=t4[:, 0 : GU - 1, :], func=COPY, scale=w1f[:, 1:2])
            nc.scalar.activation(out=bt[:, 0:GU:L, 0:nn], in_=t4[:, L - 1 : GU : L, :], func=COPY, scale=w1f[:, 1:2])

        def first_term(q, b):
            n0, nn = NBLOCKS[b]
            t4 = accs[(q, b)][:, 0 : nn * G].rearrange("p (n g) -> p g n", g=G)
            nc.vector.scalar_tensor_tensor(
                out=ot[q][:].rearrange("p m l n -> p (m l) n")[:, :, n0 : n0 + nn],
                in0=t4[:, 0:GU, :],
                scalar=w1f[:, 0:1],
                in1=bts[(q, b)][:, :, 0:nn],
                op0=MULT,
                op1=ADD,
            )

        def store(q):
            ms = slice(q * MC, (q + 1) * MC)
            nc.sync.dma_start(
                out=out[ms, :, 0, :].rearrange("m i n -> i m n"),
                in_=ot[q][:, :, L - 1, :],
            )
            nc.sync.dma_start(
                out=out[ms, :, 1:L, :].rearrange("m i l n -> i m (l n)"),
                in_=ot[q][:, :, 0 : L - 1, :].rearrange("p m l n -> p m (l n)"),
            )

        def epilogue(q):
            for b in range(len(NBLOCKS)):
                second_term(q, b)
                first_term(q, b)
            store(q)

        weights()
        for q in range(NQ + 1):
            if q < NQ:
                for mm in range(MC):
                    regroup_vector(q, mm)
                    regroup_scalar(q, mm)
                quantise_vector(q)
                quantise_scalar(q)
                for b in range(len(NBLOCKS)):
                    multiply(q, b)
            if q >= 1:
                epilogue(q - 1)
